import numpy as np
import ml_dtypes


def mxq(x, axis, fmt="e4m3"):
    dtype, down = {"e4m3": (ml_dtypes.float8_e4m3fn, 7), "e5m2": (ml_dtypes.float8_e5m2, 14)}[fmt]
    v = np.moveaxis(np.asarray(x, np.float32).astype(ml_dtypes.bfloat16).astype(np.float64), axis, -1)
    blocks = v.reshape(v.shape[:-1] + (-1, 32))
    amax = np.abs(blocks).max(-1, keepdims=True)
    byte = np.maximum(np.where(amax > 0, np.frexp(amax)[1] - 1 + 127, 0) - down, 1)
    scale = np.exp2(byte - 127.0)
    codes = (blocks / scale).astype(np.float32).astype(dtype).astype(np.float64)
    return np.moveaxis((codes * scale).reshape(v.shape), -1, axis)


WIDE = False


def mx_kscale(k):
    if not WIDE:
        return np.ones(k)
    levels = np.array([10, -10, 5, -5, 0])
    a = np.random.permutation(np.resize(levels, k // 512 * 4)).reshape(k // 512, 4)
    idx = np.arange(k)
    return np.exp2(a[idx // 512, idx % 128 // 32])


BF16 = ml_dtypes.bfloat16


def bf(x):
    return np.asarray(x, np.float32).astype(BF16)


def f64(x):
    return np.asarray(x).astype(np.float64)


B, T, D, H = 4, 256, 512, 2048
N = B * T
EMA0 = 1.0


def silu(v):
    return v / (1.0 + np.exp(-v))


def surprise_gate(err):
    err_mag = np.sqrt(np.sum(err * err)) / N
    ema = 0.95 * EMA0 + 0.05 * err_mag
    return np.minimum(err_mag / np.maximum(ema, 1e-8), 3.0)


def setup_inputs():
    s = mx_kscale(D)
    return {"x_pred": bf(np.random.standard_normal((N, D)) * s[None, :]),
            "W_gate": bf(np.random.standard_normal((H, D)) / np.sqrt(D) / s[None, :]),
            "W_up": bf(np.random.standard_normal((H, D)) / np.sqrt(D) / s[None, :]),
            "err": bf(np.random.standard_normal((N, D)) * 2.3)}


def reference(x_pred, W_gate, W_up, err):
    err = f64(err)
    sg = surprise_gate(err)
    xq = mxq(f64(x_pred), 1, "e4m3")
    gate_pre = xq @ mxq(f64(W_gate), 1, "e4m3").T
    up_pre = xq @ mxq(f64(W_up), 1, "e4m3").T
    h = silu(gate_pre) * up_pre
    grad_down = (mxq(err, 0, "e4m3").T @ mxq(h, 0, "e4m3")) / N
    return grad_down * sg

@@ -1,0 +1,224 @@
+from contextlib import ExitStack
+
+import concourse.mybir as mybir
+from concourse.masks import make_identity
+
+F32 = mybir.dt.float32
+BF16 = mybir.dt.bfloat16
+U32 = mybir.dt.uint32
+U8 = mybir.dt.uint8
+FP8X4 = mybir.dt.float8_e4m3fn_x4
+ACT = mybir.ActivationFunctionType
+ALU = mybir.AluOpType
+AXIS = mybir.AxisListType
+
+P = 128
+PACK = 4
+K_PASS = P * PACK
+BANK = 512
+
+TOKENS = 1024
+FEATURES = 512
+HIDDEN = 2048
+
+TOKEN_PASSES = TOKENS // K_PASS
+RANGES = HIDDEN // BANK
+CHUNKS = BANK // P
+FEATURE_TILES = FEATURES // P
+
+FLOPS = 2 * TOKENS * FEATURES * 2 * HIDDEN + 2 * FEATURES * TOKENS * HIDDEN
+
+
+def tile_continuummemorysystem_pb_kernel(tc, x_pred, W_gate, W_up, err, out):
+    nc = tc.nc
+    with ExitStack() as ctx:
+        ctx.enter_context(tc.manual_schedule())
+        keep = ctx.enter_context(tc.tile_pool(name="keep", bufs=1))
+        stage = ctx.enter_context(tc.tile_pool(name="stage", bufs=4))
+        psum = ctx.enter_context(tc.psum_pool(name="psum", bufs=8))
+
+        identity = keep.tile([P, P], F32)
+        make_identity(nc, identity[:])
+        ones = keep.tile([P, P], F32)
+        nc.gpsimd.memset(ones[:], 1.0)
+        half = keep.tile([P, 1], F32)
+        nc.gpsimd.memset(half[:], 0.5)
+        minus_one = keep.tile([P, 1], F32)
+        nc.gpsimd.memset(minus_one[:], -1.0)
+
+        def load_512_rows(matrix, first_row, name):
+            rows = keep.tile([P, PACK, FEATURES], BF16, name=name)
+            nc.sync.dma_start(
+                out=rows[:], in_=matrix[first_row : first_row + K_PASS, :].rearrange("(p r) d -> p r d", r=PACK)
+            )
+            return rows
+
+        x_rows = [load_512_rows(x_pred, c * K_PASS, "x_rows%d" % c) for c in range(TOKEN_PASSES)]
+        err_rows = [load_512_rows(err, c * K_PASS, "err_rows%d" % c) for c in range(TOKEN_PASSES)]
+        w_rows = [
+            [load_512_rows(weight, n * BANK, "w_rows%d_%d" % (n, kind)) for kind, weight in enumerate((W_gate, W_up))]
+            for n in range(RANGES)
+        ]
+
+        def transpose_and_quantise(rows, vector_copies, name):
+            words = rows[:].rearrange("p r d -> p (r d)").bitcast(F32)
+            grouped = stage.tile([P, BANK * PACK], BF16, tag="grouped", align_bytes=64)
+            grouped_words = grouped[:].bitcast(F32)
+            for b in range(2):
+                bank = psum.tile([P, BANK], F32, tag="bank")
+                for i in range(BANK // P):
+                    nc.tensor.transpose(
+                        out=bank[:, i * P : (i + 1) * P],
+                        in_=words[:, b * BANK + i * P : b * BANK + (i + 1) * P],
+                        identity=identity[:],
+                    )
+                src = bank[:].rearrange("p (a u m) -> p a m u", a=2, u=2)
+                dst = grouped_words[:, b * BANK : (b + 1) * BANK].rearrange("p (a m u) -> p a m u", a=2, u=2)
+                if b < vector_copies:
+                    nc.vector.tensor_copy(out=dst, in_=src)
+                else:
+                    nc.scalar.copy(out=dst, in_=src)
+            codes = keep.tile([P, BANK], U32, name=name + "_codes", align_bytes=64)
+            scales = keep.tile([P, BANK], U8, name=name + "_scales", align_bytes=64)
+            nc.vector.quantize_mx(out=codes[:].bitcast(FP8X4), scales=scales[:], in_=grouped[:])
+            return codes, scales
+
+        x_mx = [transpose_and_quantise(x_rows[c], 1, "x%d" % c) for c in range(TOKEN_PASSES)]
+
+        gram = psum.tile([P, BANK], F32, tag="bank")
+        for c in range(TOKEN_PASSES):
+            for r in range(PACK):
+                for f in range(FEATURE_TILES):
+                    block = err_rows[c][:, r, f * P : (f + 1) * P]
+                    nc.tensor.matmul(
+                        out=gram[:, 0:P],
+                        lhsT=block,
+                        rhs=block,
+                        start=(c == 0 and r == 0 and f == 0),
+                        stop=(c == TOKEN_PASSES - 1 and r == PACK - 1 and f == FEATURE_TILES - 1),
+                    )
+        err_grouped = []
+        for c in range(TOKEN_PASSES):
+            grouped = stage.tile([P, FEATURES, PACK], BF16, tag="grouped", align_bytes=64)
+            nc.vector.tensor_copy(out=grouped[:], in_=err_rows[c][:].rearrange("p r d -> p d r"))
+            err_grouped.append(grouped)
+        err_mx = []
+        for c in range(TOKEN_PASSES):
+            codes = keep.tile([P, FEATURES], U32, name="err%d_codes" % c, align_bytes=64)
+            scales = keep.tile([P, FEATURES], U8, name="err%d_scales" % c, align_bytes=64)
+            nc.vector.quantize_mx(
+                out=codes[:].bitcast(FP8X4), scales=scales[:], in_=err_grouped[c][:].rearrange("p d r -> p (d r)")
+            )
+            err_mx.append((codes, scales))
+        diagonal = keep.tile([P, P], F32)
+        nc.vector.tensor_tensor(out=diagonal[:], in0=identity[:], in1=gram[:, 0:P], op=ALU.mult)
+
+        w_mx = [
+            [transpose_and_quantise(w_rows[n][kind], 0, "w%d_%d" % (n, kind)) for kind in range(2)]
+            for n in range(RANGES)
+        ]
+
+        column_sums = psum.tile([P, BANK], F32, tag="bank")
+        nc.tensor.matmul(out=column_sums[:, 0:P], lhsT=ones[:], rhs=diagonal[:], start=True, stop=True)
+        total = keep.tile([P, 1], F32)
+        nc.vector.tensor_reduce(out=total[:], in_=column_sums[:, 0:P], axis=AXIS.X, op=ALU.add)
+        root = keep.tile([P, 1], F32)
+        nc.gpsimd.tensor_tensor(out=root[:], in0=total[:], in1=half[:], op=ALU.pow)
+        ema = keep.tile([P, 1], F32)
+        nc.gpsimd.tensor_scalar(out=ema[:], in0=root[:], scalar1=0.05 / TOKENS, scalar2=0.95, op0=ALU.mult, op1=ALU.add)
+        floored = keep.tile([P, 1], F32)
+        nc.gpsimd.tensor_scalar_max(out=floored[:], in0=ema[:], scalar1=1e-8)
+        inverse = keep.tile([P, 1], F32)
+        nc.gpsimd.tensor_tensor(out=inverse[:], in0=floored[:], in1=minus_one[:], op=ALU.pow)
+        ratio = keep.tile([P, 1], F32)
+        nc.gpsimd.tensor_tensor(out=ratio[:], in0=root[:], in1=inverse[:], op=ALU.mult)
+        gate = keep.tile([P, 1], F32)
+        nc.gpsimd.tensor_scalar(out=gate[:], in0=ratio[:], scalar1=1.0 / TOKENS, scalar2=3.0, op0=ALU.mult, op1=ALU.min)
+        scale = keep.tile([P, 1], F32)
+        nc.gpsimd.tensor_scalar_mul(out=scale[:], in0=gate[:], scalar1=1.0 / TOKENS)
+
+        def first_product(n, c, q):
+            banks = []
+            for kind in range(2):
+                bank = psum.tile([P, BANK], F32, tag="bank")
+                w_codes, w_scales = w_mx[n][kind]
+                x_codes, x_scales = x_mx[c]
+                for j in range(PACK):
+                    nc.tensor.matmul_mx(
+                        out=bank[:, j * P : (j + 1) * P],
+                        lhsT=x_codes[:, j * P : (j + 1) * P].bitcast(FP8X4),
+                        lhsT_scale=x_scales[:, j * P : (j + 1) * P],
+                        rhs=w_codes[:, q * P : (q + 1) * P].bitcast(FP8X4),
+                        rhs_scale=w_scales[:, q * P : (q + 1) * P],
+                        start=True,
+                        stop=True,
+                    )
+                banks.append(bank)
+            silu = stage.tile([P, P, PACK], F32, tag="silu")
+            nc.scalar.activation(out=silu[:], in_=banks[0][:].rearrange("p (j m) -> p m j", j=PACK), func=ACT.Silu)
+            h = stage.tile([P, P, PACK], BF16, tag="h", align_bytes=64)
+            nc.vector.tensor_tensor(
+                out=h[:], in0=silu[:], in1=banks[1][:].rearrange("p (j m) -> p m j", j=PACK), op=ALU.mult
+            )
+            return h
+
+        def evacuate(bank, n, f, on_vector):
+            result = stage.tile([P, P, CHUNKS], F32, tag="result")
+            src = bank[:].rearrange("p (q m) -> p m q", q=CHUNKS)
+            if on_vector:
+                nc.vector.tensor_scalar_mul(out=result[:], in0=src, scalar1=scale[:, 0:1])
+            else:
+                nc.scalar.activation(out=result[:], in_=src, func=ACT.Copy, scale=scale[:, 0:1])
+            nc.sync.dma_start(
+                out=out[f * P : (f + 1) * P, n * BANK : (n + 1) * BANK], in_=result[:].rearrange("p m q -> p (m q)")
+            )
+
+        def second_product_pass(bank, n, c, f):
+            err_codes, err_scales = err_mx[c]
+            h_codes, h_scales = h_mx[(n, c)]
+            nc.tensor.matmul_mx(
+                out=bank[:],
+                lhsT=err_codes[:, f * P : (f + 1) * P].bitcast(FP8X4),
+                lhsT_scale=err_scales[:, f * P : (f + 1) * P],
+                rhs=h_codes[:].bitcast(FP8X4),
+                rhs_scale=h_scales[:],
+                start=(c == 0),
+                stop=(c == TOKEN_PASSES - 1),
+            )
+
+        h_mx = {}
+
+        def quantise_h(h, n, c, q):
+            if q == 0:
+                codes = stage.tile([P, BANK], U32, tag="h_codes", align_bytes=64)
+                scales = stage.tile([P, BANK], U8, tag="h_scales", align_bytes=64)
+                h_mx[(n, c)] = (codes, scales)
+            codes, scales = h_mx[(n, c)]
+            nc.vector.quantize_mx(
+                out=codes[:, q * P : (q + 1) * P].bitcast(FP8X4),
+                scales=scales[:, q * P : (q + 1) * P],
+                in_=h[:].rearrange("p m j -> p (m j)"),
+            )
+
+        waiting = None
+        for n in range(RANGES):
+            for c in range(TOKEN_PASSES):
+                for q in range(CHUNKS):
+                    if n >= 1 and c == 1:
+                        bank = psum.tile([P, BANK], F32, tag="bank")
+                        for cc in range(TOKEN_PASSES):
+                            second_product_pass(bank, n - 1, cc, q)
+                        evacuate(bank, n - 1, q, False)
+                    h = first_product(n, c, q)
+                    if waiting is not None:
+                        quantise_h(*waiting)
+                    waiting = (h, n, c, q)
+        quantise_h(*waiting)
+
+        last = RANGES - 1
+        banks = [psum.tile([P, BANK], F32, tag="bank", name="last_bank%d" % f) for f in range(FEATURE_TILES)]
+        for c in range(TOKEN_PASSES):
+            for f in range(FEATURE_TILES):
+                second_product_pass(banks[f], last, c, f)
+        for f in range(FEATURE_TILES):
+            evacuate(banks[f], last, f, f % 2 == 1)

@@ -26,6 +26,11 @@ RANGES = HIDDEN // BANK
 CHUNKS = BANK // P
 FEATURE_TILES = FEATURES // P
 
+UNITS = RANGES * TOKEN_PASSES * CHUNKS
+PASSES = RANGES * FEATURE_TILES * TOKEN_PASSES
+LAG = 12
+H_GROUPS_ALIVE = 6
+
 FLOPS = 2 * TOKENS * FEATURES * 2 * HIDDEN + 2 * FEATURES * TOKENS * HIDDEN
 
 
@@ -137,7 +142,7 @@ def tile_continuummemorysystem_pb_kernel(tc, x_pred, W_gate, W_up, err, out):
         scale = keep.tile([P, 1], F32)
         nc.gpsimd.tensor_scalar_mul(out=scale[:], in0=gate[:], scalar1=1.0 / TOKENS)
 
-        def first_product(n, c, q):
+        def first_product(n, c, q, h):
             banks = []
             for kind in range(2):
                 bank = psum.tile([P, BANK], F32, tag="bank")
@@ -156,14 +161,12 @@ def tile_continuummemorysystem_pb_kernel(tc, x_pred, W_gate, W_up, err, out):
                 banks.append(bank)
             silu = stage.tile([P, P, PACK], F32, tag="silu")
             nc.scalar.activation(out=silu[:], in_=banks[0][:].rearrange("p (j m) -> p m j", j=PACK), func=ACT.Silu)
-            h = stage.tile([P, P, PACK], BF16, tag="h", align_bytes=64)
             nc.vector.tensor_tensor(
-                out=h[:], in0=silu[:], in1=banks[1][:].rearrange("p (j m) -> p m j", j=PACK), op=ALU.mult
+                out=h, in0=silu[:], in1=banks[1][:].rearrange("p (j m) -> p m j", j=PACK), op=ALU.mult
             )
-            return h
 
         def evacuate(bank, n, f, on_vector):
-            result = stage.tile([P, P, CHUNKS], F32, tag="result")
+            result = stage.tile([P, P, CHUNKS], F32, tag="result", bufs=8)
             src = bank[:].rearrange("p (q m) -> p m q", q=CHUNKS)
             if on_vector:
                 nc.vector.tensor_scalar_mul(out=result[:], in0=src, scalar1=scale[:, 0:1])
@@ -188,34 +191,42 @@ def tile_continuummemorysystem_pb_kernel(tc, x_pred, W_gate, W_up, err, out):
 
         h_mx = {}
 
-        def quantise_h(h, n, c, q):
-            if q == 0:
-                codes = stage.tile([P, BANK], U32, tag="h_codes", align_bytes=64)
-                scales = stage.tile([P, BANK], U8, tag="h_scales", align_bytes=64)
-                h_mx[(n, c)] = (codes, scales)
-            codes, scales = h_mx[(n, c)]
+        def quantise_h(h_grouped, n, c):
+            codes = stage.tile([P, BANK], U32, tag="h_codes", bufs=H_GROUPS_ALIVE, align_bytes=64)
+            scales = stage.tile([P, BANK], U8, tag="h_scales", bufs=H_GROUPS_ALIVE, align_bytes=64)
             nc.vector.quantize_mx(
-                out=codes[:, q * P : (q + 1) * P].bitcast(FP8X4),
-                scales=scales[:, q * P : (q + 1) * P],
-                in_=h[:].rearrange("p m j -> p (m j)"),
+                out=codes[:].bitcast(FP8X4), scales=scales[:], in_=h_grouped[:].rearrange("p m j -> p (m j)")
             )
+            h_mx[(n, c)] = (codes, scales)
+
+        open_bank = {}
+
+        def second_product_step(k, vector_helps):
+            n, rest = divmod(k, FEATURE_TILES * TOKEN_PASSES)
+            f, c = divmod(rest, TOKEN_PASSES)
+            if c == 0:
+                open_bank[f] = psum.tile([P, BANK], F32, tag="bank", name="out_bank")
+            second_product_pass(open_bank[f], n, c, f)
+            if c == TOKEN_PASSES - 1:
+                evacuate(open_bank[f], n, f, vector_helps and f % 2 == 1)
 
         waiting = None
-        for n in range(RANGES):
-            for c in range(TOKEN_PASSES):
-                for q in range(CHUNKS):
-                    if n >= 1 and c == 1:
-                        bank = psum.tile([P, BANK], F32, tag="bank")
-                        for cc in range(TOKEN_PASSES):
-                            second_product_pass(bank, n - 1, cc, q)
-                        evacuate(bank, n - 1, q, False)
-                    h = first_product(n, c, q)
-                    if waiting is not None:
-                        quantise_h(*waiting)
-                    waiting = (h, n, c, q)
+        for u in range(UNITS):
+            n, rest = divmod(u, TOKEN_PASSES * CHUNKS)
+            c, q = divmod(rest, CHUNKS)
+            if u >= LAG:
+                second_product_step(u - LAG, False)
+            if q == 0:
+                h_grouped = stage.tile([P, BANK, PACK], BF16, tag="h_grouped", align_bytes=64)
+            first_product(n, c, q, h_grouped[:, q * P : (q + 1) * P, :])
+            if q == 0 and waiting is not None:
+                quantise_h(*waiting)
+            waiting = (h_grouped, n, c)
         quantise_h(*waiting)
 
         last = RANGES - 1
+        for k in range(UNITS - LAG, last * FEATURE_TILES * TOKEN_PASSES):
+            second_product_step(k, True)
         banks = [psum.tile([P, BANK], F32, tag="bank", name="last_bank%d" % f) for f in range(FEATURE_TILES)]
         for c in range(TOKEN_PASSES):
             for f in range(FEATURE_TILES):

@@ -91,17 +91,20 @@ def tile_continuummemorysystem_pb_kernel(tc, x_pred, W_gate, W_up, err, out):
         x_mx = [transpose_and_quantise(x_rows[c], 1, "x%d" % c) for c in range(TOKEN_PASSES)]
 
         gram = psum.tile([P, BANK], F32, tag="bank")
-        for c in range(TOKEN_PASSES):
-            for r in range(PACK):
-                for f in range(FEATURE_TILES):
-                    block = err_rows[c][:, r, f * P : (f + 1) * P]
-                    nc.tensor.matmul(
-                        out=gram[:, 0:P],
-                        lhsT=block,
-                        rhs=block,
-                        start=(c == 0 and r == 0 and f == 0),
-                        stop=(c == TOKEN_PASSES - 1 and r == PACK - 1 and f == FEATURE_TILES - 1),
-                    )
+
+        def add_squares(c, r, feature_tiles):
+            for f in feature_tiles:
+                block = err_rows[c][:, r, f * P : (f + 1) * P]
+                nc.tensor.matmul(
+                    out=gram[:, 0:P],
+                    lhsT=block,
+                    rhs=block,
+                    start=(c == 0 and r == 0 and f == 0),
+                    stop=(c == TOKEN_PASSES - 1 and r == PACK - 1 and f == FEATURE_TILES - 1),
+                )
+
+        for r in range(PACK):
+            add_squares(0, r, range(FEATURE_TILES))
         err_grouped = []
         for c in range(TOKEN_PASSES):
             grouped = stage.tile([P, FEATURES, PACK], BF16, tag="grouped", align_bytes=64)
@@ -115,32 +118,40 @@ def tile_continuummemorysystem_pb_kernel(tc, x_pred, W_gate, W_up, err, out):
                 out=codes[:].bitcast(FP8X4), scales=scales[:], in_=err_grouped[c][:].rearrange("p d r -> p (d r)")
             )
             err_mx.append((codes, scales))
+        w_mx = []
+        for n in range(RANGES):
+            pair = []
+            for kind in range(2):
+                pair.append(transpose_and_quantise(w_rows[n][kind], kind, "w%d_%d" % (n, kind)))
+                add_squares(1, n, range(2 * kind, 2 * kind + 2))
+            w_mx.append(pair)
         diagonal = keep.tile([P, P], F32)
         nc.vector.tensor_tensor(out=diagonal[:], in0=identity[:], in1=gram[:, 0:P], op=ALU.mult)
 
-        w_mx = [
-            [transpose_and_quantise(w_rows[n][kind], 0, "w%d_%d" % (n, kind)) for kind in range(2)]
-            for n in range(RANGES)
-        ]
-
-        column_sums = psum.tile([P, BANK], F32, tag="bank")
-        nc.tensor.matmul(out=column_sums[:, 0:P], lhsT=ones[:], rhs=diagonal[:], start=True, stop=True)
-        total = keep.tile([P, 1], F32)
-        nc.vector.tensor_reduce(out=total[:], in_=column_sums[:, 0:P], axis=AXIS.X, op=ALU.add)
-        root = keep.tile([P, 1], F32)
-        nc.gpsimd.tensor_tensor(out=root[:], in0=total[:], in1=half[:], op=ALU.pow)
-        ema = keep.tile([P, 1], F32)
-        nc.gpsimd.tensor_scalar(out=ema[:], in0=root[:], scalar1=0.05 / TOKENS, scalar2=0.95, op0=ALU.mult, op1=ALU.add)
-        floored = keep.tile([P, 1], F32)
-        nc.gpsimd.tensor_scalar_max(out=floored[:], in0=ema[:], scalar1=1e-8)
-        inverse = keep.tile([P, 1], F32)
-        nc.gpsimd.tensor_tensor(out=inverse[:], in0=floored[:], in1=minus_one[:], op=ALU.pow)
-        ratio = keep.tile([P, 1], F32)
-        nc.gpsimd.tensor_tensor(out=ratio[:], in0=root[:], in1=inverse[:], op=ALU.mult)
-        gate = keep.tile([P, 1], F32)
-        nc.gpsimd.tensor_scalar(out=gate[:], in0=ratio[:], scalar1=1.0 / TOKENS, scalar2=3.0, op0=ALU.mult, op1=ALU.min)
         scale = keep.tile([P, 1], F32)
-        nc.gpsimd.tensor_scalar_mul(out=scale[:], in0=gate[:], scalar1=1.0 / TOKENS)
+
+        def surprise_scale():
+            column_sums = psum.tile([P, BANK], F32, tag="bank")
+            nc.tensor.matmul(out=column_sums[:, 0:P], lhsT=ones[:], rhs=diagonal[:], start=True, stop=True)
+            total = keep.tile([P, 1], F32)
+            nc.vector.tensor_reduce(out=total[:], in_=column_sums[:, 0:P], axis=AXIS.X, op=ALU.add)
+            root = keep.tile([P, 1], F32)
+            nc.gpsimd.tensor_tensor(out=root[:], in0=total[:], in1=half[:], op=ALU.pow)
+            ema = keep.tile([P, 1], F32)
+            nc.gpsimd.tensor_scalar(
+                out=ema[:], in0=root[:], scalar1=0.05 / TOKENS, scalar2=0.95, op0=ALU.mult, op1=ALU.add
+            )
+            floored = keep.tile([P, 1], F32)
+            nc.gpsimd.tensor_scalar_max(out=floored[:], in0=ema[:], scalar1=1e-8)
+            inverse = keep.tile([P, 1], F32)
+            nc.gpsimd.tensor_tensor(out=inverse[:], in0=floored[:], in1=minus_one[:], op=ALU.pow)
+            ratio = keep.tile([P, 1], F32)
+            nc.gpsimd.tensor_tensor(out=ratio[:], in0=root[:], in1=inverse[:], op=ALU.mult)
+            gate = keep.tile([P, 1], F32)
+            nc.gpsimd.tensor_scalar(
+                out=gate[:], in0=ratio[:], scalar1=1.0 / TOKENS, scalar2=3.0, op0=ALU.mult, op1=ALU.min
+            )
+            nc.gpsimd.tensor_scalar_mul(out=scale[:], in0=gate[:], scalar1=1.0 / TOKENS)
 
         def first_product(n, c, q, h):
             banks = []
@@ -216,6 +227,8 @@ def tile_continuummemorysystem_pb_kernel(tc, x_pred, W_gate, W_up, err, out):
             c, q = divmod(rest, CHUNKS)
             if u >= LAG:
                 second_product_step(u - LAG, False)
+            if u == CHUNKS:
+                surprise_scale()
             if q == 0:
                 h_grouped = stage.tile([P, BANK, PACK], BF16, tag="h_grouped", align_bytes=64)
             first_product(n, c, q, h_grouped[:, q * P : (q + 1) * P, :])

@@ -22,14 +22,13 @@ FEATURES = 512
 HIDDEN = 2048
 
 TOKEN_PASSES = TOKENS // K_PASS
-RANGES = HIDDEN // BANK
-CHUNKS = BANK // P
+RANGE = 2 * P
+RANGES = HIDDEN // RANGE
+CHUNKS = RANGE // P
 FEATURE_TILES = FEATURES // P
-
-UNITS = RANGES * TOKEN_PASSES * CHUNKS
-PASSES = RANGES * FEATURE_TILES * TOKEN_PASSES
+SLOTS = TOKEN_PASSES * CHUNKS
+CATCH_UP = 6
 LAG = 12
-H_GROUPS_ALIVE = 6
 
 FLOPS = 2 * TOKENS * FEATURES * 2 * HIDDEN + 2 * FEATURES * TOKENS * HIDDEN
 
@@ -40,7 +39,7 @@ def tile_continuummemorysystem_pb_kernel(tc, x_pred, W_gate, W_up, err, out):
         ctx.enter_context(tc.manual_schedule())
         keep = ctx.enter_context(tc.tile_pool(name="keep", bufs=1))
         stage = ctx.enter_context(tc.tile_pool(name="stage", bufs=4))
-        psum = ctx.enter_context(tc.psum_pool(name="psum", bufs=8))
+        psum = ctx.enter_context(tc.psum_pool(name="psum", bufs=2))
 
         identity = keep.tile([P, P], F32)
         make_identity(nc, identity[:])
@@ -51,147 +50,153 @@ def tile_continuummemorysystem_pb_kernel(tc, x_pred, W_gate, W_up, err, out):
         minus_one = keep.tile([P, 1], F32)
         nc.gpsimd.memset(minus_one[:], -1.0)
 
-        def load_512_rows(matrix, first_row, name):
-            rows = keep.tile([P, PACK, FEATURES], BF16, name=name)
-            nc.sync.dma_start(
-                out=rows[:], in_=matrix[first_row : first_row + K_PASS, :].rearrange("(p r) d -> p r d", r=PACK)
-            )
+        def load(view, slots, name):
+            rows = keep.tile([P, slots, FEATURES], BF16, name=name)
+            nc.sync.dma_start(out=rows[:], in_=view)
             return rows
 
-        x_rows = [load_512_rows(x_pred, c * K_PASS, "x_rows%d" % c) for c in range(TOKEN_PASSES)]
-        err_rows = [load_512_rows(err, c * K_PASS, "err_rows%d" % c) for c in range(TOKEN_PASSES)]
-        w_rows = [
-            [load_512_rows(weight, n * BANK, "w_rows%d_%d" % (n, kind)) for kind, weight in enumerate((W_gate, W_up))]
-            for n in range(RANGES)
-        ]
+        def load_x(c):
+            view = x_pred[c * K_PASS : (c + 1) * K_PASS, :].rearrange("(p r) d -> p r d", r=PACK)
+            return [load(view[:, 2 * b : 2 * b + 2, :], 2, "x_rows%d_%d" % (c, b)) for b in range(2)]
 
-        def transpose_and_quantise(rows, vector_copies, name):
+        def load_w(i):
+            return [
+                load(weight[i * RANGE : (i + 1) * RANGE, :].rearrange("(p r) d -> p r d", r=CHUNKS), CHUNKS, "w_rows%d_%d" % (i, kind))
+                for kind, weight in enumerate((W_gate, W_up))
+            ]
+
+        def load_err(c):
+            view = err[c * K_PASS : (c + 1) * K_PASS, :].rearrange("(p r) d -> p r d", r=PACK)
+            return load(view, PACK, "err_rows%d" % c)
+
+        x_rows = [load_x(0)]
+        w_rows = [load_w(0)]
+        x_rows.append(load_x(1))
+        w_rows.append(load_w(1))
+        err_rows = [load_err(c) for c in range(TOKEN_PASSES)]
+        for i in range(2, RANGES):
+            w_rows.append(load_w(i))
+
+        def transpose_rows(rows, tag):
             words = rows[:].rearrange("p r d -> p (r d)").bitcast(F32)
-            grouped = stage.tile([P, BANK * PACK], BF16, tag="grouped", align_bytes=64)
-            grouped_words = grouped[:].bitcast(F32)
-            for b in range(2):
-                bank = psum.tile([P, BANK], F32, tag="bank")
-                for i in range(BANK // P):
-                    nc.tensor.transpose(
-                        out=bank[:, i * P : (i + 1) * P],
-                        in_=words[:, b * BANK + i * P : b * BANK + (i + 1) * P],
-                        identity=identity[:],
-                    )
-                src = bank[:].rearrange("p (a u m) -> p a m u", a=2, u=2)
-                dst = grouped_words[:, b * BANK : (b + 1) * BANK].rearrange("p (a m u) -> p a m u", a=2, u=2)
-                if b < vector_copies:
-                    nc.vector.tensor_copy(out=dst, in_=src)
-                else:
-                    nc.scalar.copy(out=dst, in_=src)
+            bank = psum.tile([P, BANK], F32, tag=tag, name="bank")
+            for i in range(BANK // P):
+                nc.tensor.transpose(
+                    out=bank[:, i * P : (i + 1) * P], in_=words[:, i * P : (i + 1) * P], identity=identity[:]
+                )
+            return bank
+
+        def copy_out(bank, on_vector):
+            grouped = stage.tile([P, BANK * 2], BF16, tag="grouped", name="grouped", align_bytes=64)
+            src = bank[:].rearrange("p (a u m) -> p a m u", a=2, u=2)
+            dst = grouped[:].bitcast(F32).rearrange("p (a m u) -> p a m u", a=2, u=2)
+            if on_vector:
+                nc.vector.tensor_copy(out=dst, in_=src)
+            else:
+                nc.scalar.copy(out=dst, in_=src)
+            return grouped
+
+        def quantise(grouped, codes, scales):
+            nc.vector.quantize_mx(out=codes.bitcast(FP8X4), scales=scales, in_=grouped)
+
+        def code_tiles(name):
             codes = keep.tile([P, BANK], U32, name=name + "_codes", align_bytes=64)
             scales = keep.tile([P, BANK], U8, name=name + "_scales", align_bytes=64)
-            nc.vector.quantize_mx(out=codes[:].bitcast(FP8X4), scales=scales[:], in_=grouped[:])
             return codes, scales
 
-        x_mx = [transpose_and_quantise(x_rows[c], 1, "x%d" % c) for c in range(TOKEN_PASSES)]
+        x_mx = [code_tiles("x%d" % c) for c in range(TOKEN_PASSES)]
+        w_mx = [code_tiles("w%d" % i) for i in range(RANGES)]
+        err_mx = [code_tiles("err%d" % c) for c in range(TOKEN_PASSES)]
 
-        gram = psum.tile([P, BANK], F32, tag="bank")
+        def quantise_half(grouped, pair, b):
+            codes, scales = pair
+            quantise(grouped[:], codes[:, b * RANGE : (b + 1) * RANGE], scales[:, b * RANGE : (b + 1) * RANGE])
 
-        def add_squares(c, r, feature_tiles):
-            for f in feature_tiles:
+        x0 = [transpose_rows(x_rows[0][b], "trans") for b in range(2)]
+        x0_grouped = [copy_out(x0[b], b == 0) for b in range(2)]
+        w0 = [transpose_rows(w_rows[0][b], "out") for b in range(2)]
+        x1 = [transpose_rows(x_rows[1][b], "up") for b in range(2)]
+        w0_grouped = [copy_out(w0[b], False) for b in range(2)]
+        for b in range(2):
+            quantise_half(x0_grouped[b], x_mx[0], b)
+        quantise_half(w0_grouped[0], w_mx[0], 0)
+        x1_grouped = [copy_out(x1[b], b == 0) for b in range(2)]
+        quantise_half(w0_grouped[1], w_mx[0], 1)
+        for b in range(2):
+            quantise_half(x1_grouped[b], x_mx[1], b)
+
+        err_grouped = [stage.tile([P, FEATURES, PACK], BF16, tag="err_grouped", name="err_grouped%d" % c, align_bytes=64) for c in range(TOKEN_PASSES)]
+
+        def interleave_err(c, piece, pieces):
+            width = FEATURES // pieces
+            d = piece * width
+            dst = err_grouped[c][:, d : d + width, :]
+            src = err_rows[c][:, :, d : d + width].rearrange("p r d -> p d r")
+            nc.gpsimd.tensor_scalar(out=dst, in0=src, scalar1=1.0, scalar2=0.0, op0=ALU.mult, op1=ALU.add)
+
+        gram_blocks = [(c, r, f) for c in range(TOKEN_PASSES) for r in range(PACK) for f in range(FEATURE_TILES)]
+        gram = []
+
+        def add_squares(first, last):
+            if not gram:
+                gram.append(psum.tile([P, BANK], F32, tag="out", name="gram"))
+            for k in range(first, last):
+                c, r, f = gram_blocks[k]
                 block = err_rows[c][:, r, f * P : (f + 1) * P]
                 nc.tensor.matmul(
-                    out=gram[:, 0:P],
-                    lhsT=block,
-                    rhs=block,
-                    start=(c == 0 and r == 0 and f == 0),
-                    stop=(c == TOKEN_PASSES - 1 and r == PACK - 1 and f == FEATURE_TILES - 1),
+                    out=gram[0][:, 0:P], lhsT=block, rhs=block, start=(k == 0), stop=(k == len(gram_blocks) - 1)
                 )
 
-        for r in range(PACK):
-            add_squares(0, r, range(FEATURE_TILES))
-        err_grouped = []
-        for c in range(TOKEN_PASSES):
-            grouped = stage.tile([P, FEATURES, PACK], BF16, tag="grouped", align_bytes=64)
-            nc.vector.tensor_copy(out=grouped[:], in_=err_rows[c][:].rearrange("p r d -> p d r"))
-            err_grouped.append(grouped)
-        err_mx = []
-        for c in range(TOKEN_PASSES):
-            codes = keep.tile([P, FEATURES], U32, name="err%d_codes" % c, align_bytes=64)
-            scales = keep.tile([P, FEATURES], U8, name="err%d_scales" % c, align_bytes=64)
-            nc.vector.quantize_mx(
-                out=codes[:].bitcast(FP8X4), scales=scales[:], in_=err_grouped[c][:].rearrange("p d r -> p (d r)")
-            )
-            err_mx.append((codes, scales))
-        w_mx = []
-        for n in range(RANGES):
-            pair = []
-            for kind in range(2):
-                pair.append(transpose_and_quantise(w_rows[n][kind], kind, "w%d_%d" % (n, kind)))
-                add_squares(1, n, range(2 * kind, 2 * kind + 2))
-            w_mx.append(pair)
         diagonal = keep.tile([P, P], F32)
-        nc.vector.tensor_tensor(out=diagonal[:], in0=identity[:], in1=gram[:, 0:P], op=ALU.mult)
-
         scale = keep.tile([P, 1], F32)
 
         def surprise_scale():
-            column_sums = psum.tile([P, BANK], F32, tag="bank")
-            nc.tensor.matmul(out=column_sums[:, 0:P], lhsT=ones[:], rhs=diagonal[:], start=True, stop=True)
+            column_sums = gram[0][:, P : 2 * P]
+            nc.tensor.matmul(out=column_sums, lhsT=ones[:], rhs=diagonal[:], start=True, stop=True)
             total = keep.tile([P, 1], F32)
-            nc.vector.tensor_reduce(out=total[:], in_=column_sums[:, 0:P], axis=AXIS.X, op=ALU.add)
+            nc.vector.tensor_reduce(out=total[:], in_=column_sums, axis=AXIS.X, op=ALU.add)
             root = keep.tile([P, 1], F32)
             nc.gpsimd.tensor_tensor(out=root[:], in0=total[:], in1=half[:], op=ALU.pow)
             ema = keep.tile([P, 1], F32)
             nc.gpsimd.tensor_scalar(
                 out=ema[:], in0=root[:], scalar1=0.05 / TOKENS, scalar2=0.95, op0=ALU.mult, op1=ALU.add
             )
-            floored = keep.tile([P, 1], F32)
-            nc.gpsimd.tensor_scalar_max(out=floored[:], in0=ema[:], scalar1=1e-8)
             inverse = keep.tile([P, 1], F32)
-            nc.gpsimd.tensor_tensor(out=inverse[:], in0=floored[:], in1=minus_one[:], op=ALU.pow)
+            nc.gpsimd.tensor_tensor(out=inverse[:], in0=ema[:], in1=minus_one[:], op=ALU.pow)
             ratio = keep.tile([P, 1], F32)
             nc.gpsimd.tensor_tensor(out=ratio[:], in0=root[:], in1=inverse[:], op=ALU.mult)
-            gate = keep.tile([P, 1], F32)
             nc.gpsimd.tensor_scalar(
-                out=gate[:], in0=ratio[:], scalar1=1.0 / TOKENS, scalar2=3.0, op0=ALU.mult, op1=ALU.min
-            )
-            nc.gpsimd.tensor_scalar_mul(out=scale[:], in0=gate[:], scalar1=1.0 / TOKENS)
-
-        def first_product(n, c, q, h):
-            banks = []
-            for kind in range(2):
-                bank = psum.tile([P, BANK], F32, tag="bank")
-                w_codes, w_scales = w_mx[n][kind]
-                x_codes, x_scales = x_mx[c]
-                for j in range(PACK):
-                    nc.tensor.matmul_mx(
-                        out=bank[:, j * P : (j + 1) * P],
-                        lhsT=x_codes[:, j * P : (j + 1) * P].bitcast(FP8X4),
-                        lhsT_scale=x_scales[:, j * P : (j + 1) * P],
-                        rhs=w_codes[:, q * P : (q + 1) * P].bitcast(FP8X4),
-                        rhs_scale=w_scales[:, q * P : (q + 1) * P],
-                        start=True,
-                        stop=True,
-                    )
-                banks.append(bank)
-            silu = stage.tile([P, P, PACK], F32, tag="silu")
-            nc.scalar.activation(out=silu[:], in_=banks[0][:].rearrange("p (j m) -> p m j", j=PACK), func=ACT.Silu)
-            nc.vector.tensor_tensor(
-                out=h, in0=silu[:], in1=banks[1][:].rearrange("p (j m) -> p m j", j=PACK), op=ALU.mult
+                out=scale[:], in0=ratio[:], scalar1=1.0 / TOKENS**2, scalar2=3.0 / TOKENS, op0=ALU.mult, op1=ALU.min
             )
 
-        def evacuate(bank, n, f, on_vector):
-            result = stage.tile([P, P, CHUNKS], F32, tag="result", bufs=8)
-            src = bank[:].rearrange("p (q m) -> p m q", q=CHUNKS)
-            if on_vector:
-                nc.vector.tensor_scalar_mul(out=result[:], in0=src, scalar1=scale[:, 0:1])
-            else:
-                nc.scalar.activation(out=result[:], in_=src, func=ACT.Copy, scale=scale[:, 0:1])
-            nc.sync.dma_start(
-                out=out[f * P : (f + 1) * P, n * BANK : (n + 1) * BANK], in_=result[:].rearrange("p m q -> p (m q)")
-            )
+        def product(bank, pair, c, w, q, kind):
+            codes, scales = w
+            x_codes, x_scales = pair
+            first = kind * RANGE + q * P
+            for j in range(PACK):
+                nc.tensor.matmul_mx(
+                    out=bank[:, j * P : (j + 1) * P],
+                    lhsT=x_codes[:, j * P : (j + 1) * P].bitcast(FP8X4),
+                    lhsT_scale=x_scales[:, j * P : (j + 1) * P],
+                    rhs=codes[:, first : first + P].bitcast(FP8X4),
+                    rhs_scale=scales[:, first : first + P],
+                    start=True,
+                    stop=True,
+                )
 
-        def second_product_pass(bank, n, c, f):
+        h_mx = {}
+
+        def quantise_h(h_grouped, i, c):
+            codes = stage.tile([P, RANGE], U32, tag="h_codes", bufs=10, align_bytes=64)
+            scales = stage.tile([P, RANGE], U8, tag="h_scales", bufs=10, align_bytes=64)
+            quantise(h_grouped[:].rearrange("p m j -> p (m j)"), codes[:], scales[:])
+            h_mx[(i, c)] = (codes, scales)
+
+        def second_pass(target, i, c, f):
             err_codes, err_scales = err_mx[c]
-            h_codes, h_scales = h_mx[(n, c)]
+            h_codes, h_scales = h_mx[(i, c)]
             nc.tensor.matmul_mx(
-                out=bank[:],
+                out=target,
                 lhsT=err_codes[:, f * P : (f + 1) * P].bitcast(FP8X4),
                 lhsT_scale=err_scales[:, f * P : (f + 1) * P],
                 rhs=h_codes[:].bitcast(FP8X4),
@@ -200,49 +205,133 @@ def tile_continuummemorysystem_pb_kernel(tc, x_pred, W_gate, W_up, err, out):
                 stop=(c == TOKEN_PASSES - 1),
             )
 
-        h_mx = {}
+        out_banks = {}
 
-        def quantise_h(h_grouped, n, c):
-            codes = stage.tile([P, BANK], U32, tag="h_codes", bufs=H_GROUPS_ALIVE, align_bytes=64)
-            scales = stage.tile([P, BANK], U8, tag="h_scales", bufs=H_GROUPS_ALIVE, align_bytes=64)
-            nc.vector.quantize_mx(
-                out=codes[:].bitcast(FP8X4), scales=scales[:], in_=h_grouped[:].rearrange("p m j -> p (m j)")
+        def second_group(k, tag="out"):
+            i, f = divmod(k, FEATURE_TILES)
+            b, half_bank = divmod(f, 2)
+            if half_bank == 0:
+                out_banks[(i, b)] = psum.tile([P, BANK], F32, tag=tag, name="out_bank")
+            for c in range(TOKEN_PASSES):
+                second_pass(out_banks[(i, b)][:, half_bank * RANGE : (half_bank + 1) * RANGE], i, c, f)
+
+        def scaled(dst, src, on_vector):
+            if on_vector:
+                nc.vector.tensor_scalar_mul(out=dst, in0=src, scalar1=scale[:, 0:1])
+            else:
+                nc.scalar.activation(out=dst, in_=src, func=ACT.Copy, scale=scale[:, 0:1])
+
+        def evacuate(i, b, on_vector):
+            result = stage.tile([P, 2, P, CHUNKS], F32, tag="result", bufs=4)
+            src = out_banks[(i, b)][:].rearrange("p (f q m) -> p f m q", f=2, q=CHUNKS)
+            scaled(result[:], src, on_vector)
+            nc.sync.dma_start(
+                out=out[2 * b * P : 2 * (b + 1) * P, i * RANGE : (i + 1) * RANGE].rearrange("(f p) n -> p f n", f=2),
+                in_=result[:].rearrange("p f m q -> p f (m q)"),
             )
-            h_mx[(n, c)] = (codes, scales)
 
-        open_bank = {}
+        UNITS = RANGES * SLOTS
+        LAST = RANGES - 1
 
-        def second_product_step(k, vector_helps):
-            n, rest = divmod(k, FEATURE_TILES * TOKEN_PASSES)
-            f, c = divmod(rest, TOKEN_PASSES)
-            if c == 0:
-                open_bank[f] = psum.tile([P, BANK], F32, tag="bank", name="out_bank")
-            second_product_pass(open_bank[f], n, c, f)
-            if c == TOKEN_PASSES - 1:
-                evacuate(open_bank[f], n, f, vector_helps and f % 2 == 1)
+        def place(u):
+            i, slot = divmod(u, SLOTS)
+            return (i,) + divmod(slot, CHUNKS)
+
+        def unit_product(u, kind):
+            i, c, q = place(u)
+            bank = psum.tile([P, BANK], F32, tag=("gate", "up")[kind], name="bank")
+            product(bank, x_mx[c], c, w_mx[i], q, kind)
+            return bank
+
+        def unit_silu(bank):
+            silu = stage.tile([P, P, PACK], F32, tag="silu", name="silu")
+            nc.scalar.activation(out=silu[:], in_=bank[:].rearrange("p (j m) -> p m j", j=PACK), func=ACT.Silu)
+            return silu
+
+        w_start = {1: 1}
+        for t in range(2, RANGES):
+            w_start[SLOTS * (t - 2) + 3] = t
+
+        def groups(u):
+            first = u - LAG + max(0, u - (UNITS - CATCH_UP))
+            return [k for k in range(first, first + (2 if u >= UNITS - CATCH_UP else 1)) if k >= 0]
 
         waiting = None
+        to_quantise = []
+        w_banks = []
+        gate_bank = unit_product(0, 0)
+        silu = unit_silu(gate_bank)
         for u in range(UNITS):
-            n, rest = divmod(u, TOKEN_PASSES * CHUNKS)
-            c, q = divmod(rest, CHUNKS)
-            if u >= LAG:
-                second_product_step(u - LAG, False)
-            if u == CHUNKS:
+            i, c, q = place(u)
+            slot = c * CHUNKS + q
+            if u == 1:
+                up_bank = unit_product(u, 1)
+                w_banks = [transpose_rows(w_rows[1][b], "trans") for b in range(2)]
+            if u + 1 < UNITS:
+                gate_bank = unit_product(u + 1, 0)
+            if u in w_start and u > 1:
+                w_banks = [transpose_rows(w_rows[w_start[u]][b], "trans") for b in range(2)]
+            for k in groups(u):
+                second_group(k)
+            if u == 10:
                 surprise_scale()
+            if u != 1:
+                up_bank = unit_product(u, 1)
+            if 2 <= u < 8:
+                add_squares(32 * (u - 2) // 6, 32 * (u - 1) // 6)
+            ready = to_quantise
+            if u != 1:
+                next_silu = unit_silu(gate_bank) if u + 1 < UNITS else None
+            to_quantise = []
+            for b in range(2):
+                if (u if w_start.get(u) == 1 else u - b) in w_start and not (b == 1 and u == 2):
+                    to_quantise.append((copy_out(w_banks[b], u == 1 and b == 1), w_start[u if u == 1 else u - b], b))
+            for k in groups(u):
+                if k % FEATURE_TILES == 1:
+                    evacuate(k // FEATURE_TILES, 0, False)
+            if u == 1:
+                next_silu = unit_silu(gate_bank)
+            if u == 2:
+                for c_err in range(TOKEN_PASSES):
+                    for piece in range(8):
+                        interleave_err(c_err, piece, 8)
+            for k in groups(u):
+                if k % FEATURE_TILES == 3:
+                    evacuate(k // FEATURE_TILES, 1, True)
             if q == 0:
-                h_grouped = stage.tile([P, BANK, PACK], BF16, tag="h_grouped", align_bytes=64)
-            first_product(n, c, q, h_grouped[:, q * P : (q + 1) * P, :])
+                h_grouped = stage.tile([P, RANGE, PACK], BF16, tag="h_grouped", align_bytes=64)
+            if u == 8:
+                nc.vector.tensor_tensor(out=diagonal[:], in0=identity[:], in1=gram[0][:, 0:P], op=ALU.mult)
+            for grouped, t, b in ready:
+                quantise_half(grouped, w_mx[t], b)
+            nc.vector.tensor_tensor(
+                out=h_grouped[:, q * P : (q + 1) * P, :],
+                in0=silu[:],
+                in1=up_bank[:].rearrange("p (j m) -> p m j", j=PACK),
+                op=ALU.mult,
+            )
+            silu = next_silu
             if q == 0 and waiting is not None:
                 quantise_h(*waiting)
-            waiting = (h_grouped, n, c)
-        quantise_h(*waiting)
-
-        last = RANGES - 1
-        for k in range(UNITS - LAG, last * FEATURE_TILES * TOKEN_PASSES):
-            second_product_step(k, True)
-        banks = [psum.tile([P, BANK], F32, tag="bank", name="last_bank%d" % f) for f in range(FEATURE_TILES)]
-        for c in range(TOKEN_PASSES):
-            for f in range(FEATURE_TILES):
-                second_product_pass(banks[f], last, c, f)
+            waiting = (h_grouped, i, c)
+            if u in (6, 8):
+                c_err = (u - 6) // 2
+                quantise(err_grouped[c_err][:].rearrange("p d r -> p (d r)"), err_mx[c_err][0][:], err_mx[c_err][1][:])
+        for k in range(UNITS - LAG + CATCH_UP, LAST * FEATURE_TILES):
+            second_group(k, "trans" if k >= LAST * FEATURE_TILES - 2 else "out")
+            if k % FEATURE_TILES == 1:
+                evacuate(k // FEATURE_TILES, 0, False)
+        last_banks = [psum.tile([P, BANK], F32, tag=("trans", "gate", "gate", "out")[f], name="last_bank%d" % f) for f in range(FEATURE_TILES)]
         for f in range(FEATURE_TILES):
-            evacuate(banks[f], last, f, f % 2 == 1)
+            second_pass(last_banks[f][:, 0:RANGE], LAST, 0, f)
+        quantise_h(*waiting)
+        evacuate(LAST - 1, 1, False)
+        for f in range(FEATURE_TILES):
+            second_pass(last_banks[f][:, 0:RANGE], LAST, 1, f)
+        for f in range(FEATURE_TILES):
+            result = stage.tile([P, P, CHUNKS], F32, tag="last_result")
+            scaled(result[:], last_banks[f][:, 0:RANGE].rearrange("p (q m) -> p m q", q=CHUNKS), f % 2 == 1)
+            nc.sync.dma_start(
+                out=out[f * P : (f + 1) * P, LAST * RANGE : (LAST + 1) * RANGE],
+                in_=result[:].rearrange("p m q -> p (m q)"),
+            )

@@ -132,7 +132,10 @@ def tile_continuummemorysystem_pb_kernel(tc, x_pred, W_gate, W_up, err, out):
             d = piece * width
             dst = err_grouped[c][:, d : d + width, :]
             src = err_rows[c][:, :, d : d + width].rearrange("p r d -> p d r")
-            nc.gpsimd.tensor_scalar(out=dst, in0=src, scalar1=1.0, scalar2=0.0, op0=ALU.mult, op1=ALU.add)
+            if c == 0:
+                nc.vector.tensor_copy(out=dst, in_=src)
+            else:
+                nc.scalar.copy(out=dst, in_=src)
 
         gram_blocks = [(c, r, f) for c in range(TOKEN_PASSES) for r in range(PACK) for f in range(FEATURE_TILES)]
         gram = []
@@ -291,10 +294,9 @@ def tile_continuummemorysystem_pb_kernel(tc, x_pred, W_gate, W_up, err, out):
                     evacuate(k // FEATURE_TILES, 0, False)
             if u == 1:
                 next_silu = unit_silu(gate_bank)
-            if u == 2:
-                for c_err in range(TOKEN_PASSES):
-                    for piece in range(8):
-                        interleave_err(c_err, piece, 8)
+            if 3 <= u < 7:
+                interleave_err(1, u - 3, 4)
+                interleave_err(0, u - 3, 4)
             for k in groups(u):
                 if k % FEATURE_TILES == 3:
                     evacuate(k // FEATURE_TILES, 1, True)
@@ -314,8 +316,8 @@ def tile_continuummemorysystem_pb_kernel(tc, x_pred, W_gate, W_up, err, out):
             if q == 0 and waiting is not None:
                 quantise_h(*waiting)
             waiting = (h_grouped, i, c)
-            if u in (6, 8):
-                c_err = (u - 6) // 2
+            if u in (8, 9):
+                c_err = u - 8
                 quantise(err_grouped[c_err][:].rearrange("p d r -> p (d r)"), err_mx[c_err][0][:], err_mx[c_err][1][:])
         for k in range(UNITS - LAG + CATCH_UP, LAST * FEATURE_TILES):
             second_group(k, "trans" if k >= LAST * FEATURE_TILES - 2 else "out")

@@ -28,6 +28,7 @@ CHUNKS = RANGE // P
 FEATURE_TILES = FEATURES // P
 SLOTS = TOKEN_PASSES * CHUNKS
 CATCH_UP = 6
+WARM = 4
 LAG = 12
 
 FLOPS = 2 * TOKENS * FEATURES * 2 * HIDDEN + 2 * FEATURES * TOKENS * HIDDEN
@@ -49,6 +50,9 @@ def tile_continuummemorysystem_pb_kernel(tc, x_pred, W_gate, W_up, err, out):
         nc.gpsimd.memset(half[:], 0.5)
         minus_one = keep.tile([P, 1], F32)
         nc.gpsimd.memset(minus_one[:], -1.0)
+
+        warm = keep.tile([P, BANK], BF16)
+        nc.vector.memset(warm[:], 0.0)
 
         def load(view, slots, name):
             rows = keep.tile([P, slots, FEATURES], BF16, name=name)
@@ -112,6 +116,9 @@ def tile_continuummemorysystem_pb_kernel(tc, x_pred, W_gate, W_up, err, out):
             codes, scales = pair
             quantise(grouped[:], codes[:, b * RANGE : (b + 1) * RANGE], scales[:, b * RANGE : (b + 1) * RANGE])
 
+        warm_bank = psum.tile([P, BANK], F32, tag="gate", name="warm_bank")
+        for i in range(WARM):
+            nc.tensor.matmul(out=warm_bank[:], lhsT=warm[:, 0:P], rhs=warm[:], start=True, stop=True)
         x0 = [transpose_rows(x_rows[0][b], "trans") for b in range(2)]
         x0_grouped = [copy_out(x0[b], b == 0) for b in range(2)]
         w0 = [transpose_rows(w_rows[0][b], "out") for b in range(2)]

@@ -27,8 +27,10 @@ RANGES = HIDDEN // RANGE
 CHUNKS = RANGE // P
 FEATURE_TILES = FEATURES // P
 SLOTS = TOKEN_PASSES * CHUNKS
-CATCH_UP = 6
+CATCH_UP = 4
 WARM = 4
+UNIT_BANKS = 5
+BUFS = {"side": 3, "unit": UNIT_BANKS}
 LAG = 12
 
 FLOPS = 2 * TOKENS * FEATURES * 2 * HIDDEN + 2 * FEATURES * TOKENS * HIDDEN
@@ -40,7 +42,7 @@ def tile_continuummemorysystem_pb_kernel(tc, x_pred, W_gate, W_up, err, out):
         ctx.enter_context(tc.manual_schedule())
         keep = ctx.enter_context(tc.tile_pool(name="keep", bufs=1))
         stage = ctx.enter_context(tc.tile_pool(name="stage", bufs=4))
-        psum = ctx.enter_context(tc.psum_pool(name="psum", bufs=2))
+        psum = ctx.enter_context(tc.psum_pool(name="psum", bufs=1))
 
         identity = keep.tile([P, P], F32)
         make_identity(nc, identity[:])
@@ -83,7 +85,7 @@ def tile_continuummemorysystem_pb_kernel(tc, x_pred, W_gate, W_up, err, out):
 
         def transpose_rows(rows, tag):
             words = rows[:].rearrange("p r d -> p (r d)").bitcast(F32)
-            bank = psum.tile([P, BANK], F32, tag=tag, name="bank")
+            bank = psum.tile([P, BANK], F32, tag=tag, bufs=BUFS[tag], name="bank")
             for i in range(BANK // P):
                 nc.tensor.transpose(
                     out=bank[:, i * P : (i + 1) * P], in_=words[:, i * P : (i + 1) * P], identity=identity[:]
@@ -116,13 +118,13 @@ def tile_continuummemorysystem_pb_kernel(tc, x_pred, W_gate, W_up, err, out):
             codes, scales = pair
             quantise(grouped[:], codes[:, b * RANGE : (b + 1) * RANGE], scales[:, b * RANGE : (b + 1) * RANGE])
 
-        warm_bank = psum.tile([P, BANK], F32, tag="gate", name="warm_bank")
+        warm_bank = psum.tile([P, BANK], F32, tag="unit", bufs=UNIT_BANKS, name="warm_bank")
         for i in range(WARM):
             nc.tensor.matmul(out=warm_bank[:], lhsT=warm[:, 0:P], rhs=warm[:], start=True, stop=True)
-        x0 = [transpose_rows(x_rows[0][b], "trans") for b in range(2)]
+        x0 = [transpose_rows(x_rows[0][b], "side") for b in range(2)]
         x0_grouped = [copy_out(x0[b], b == 0) for b in range(2)]
-        w0 = [transpose_rows(w_rows[0][b], "out") for b in range(2)]
-        x1 = [transpose_rows(x_rows[1][b], "up") for b in range(2)]
+        w0 = [transpose_rows(w_rows[0][b], "unit") for b in range(2)]
+        x1 = [transpose_rows(x_rows[1][b], "unit") for b in range(2)]
         w0_grouped = [copy_out(w0[b], False) for b in range(2)]
         for b in range(2):
             quantise_half(x0_grouped[b], x_mx[0], b)
@@ -149,7 +151,7 @@ def tile_continuummemorysystem_pb_kernel(tc, x_pred, W_gate, W_up, err, out):
 
         def add_squares(first, last):
             if not gram:
-                gram.append(psum.tile([P, BANK], F32, tag="out", name="gram"))
+                gram.append(psum.tile([P, BANK], F32, tag="side", bufs=3, name="gram"))
             for k in range(first, last):
                 c, r, f = gram_blocks[k]
                 block = err_rows[c][:, r, f * P : (f + 1) * P]
@@ -161,7 +163,8 @@ def tile_continuummemorysystem_pb_kernel(tc, x_pred, W_gate, W_up, err, out):
         scale = keep.tile([P, 1], F32)
 
         def surprise_scale():
-            column_sums = gram[0][:, P : 2 * P]
+            sums_bank = psum.tile([P, BANK], F32, tag="unit", bufs=UNIT_BANKS, name="sums_bank")
+            column_sums = sums_bank[:, 0:P]
             nc.tensor.matmul(out=column_sums, lhsT=ones[:], rhs=diagonal[:], start=True, stop=True)
             total = keep.tile([P, 1], F32)
             nc.vector.tensor_reduce(out=total[:], in_=column_sums, axis=AXIS.X, op=ALU.add)
@@ -217,11 +220,11 @@ def tile_continuummemorysystem_pb_kernel(tc, x_pred, W_gate, W_up, err, out):
 
         out_banks = {}
 
-        def second_group(k, tag="out"):
+        def second_group(k, tag="side"):
             i, f = divmod(k, FEATURE_TILES)
             b, half_bank = divmod(f, 2)
             if half_bank == 0:
-                out_banks[(i, b)] = psum.tile([P, BANK], F32, tag=tag, name="out_bank")
+                out_banks[(i, b)] = psum.tile([P, BANK], F32, tag=tag, bufs=BUFS[tag], name="out_bank")
             for c in range(TOKEN_PASSES):
                 second_pass(out_banks[(i, b)][:, half_bank * RANGE : (half_bank + 1) * RANGE], i, c, f)
 
@@ -249,7 +252,7 @@ def tile_continuummemorysystem_pb_kernel(tc, x_pred, W_gate, W_up, err, out):
 
         def unit_product(u, kind):
             i, c, q = place(u)
-            bank = psum.tile([P, BANK], F32, tag=("gate", "up")[kind], name="bank")
+            bank = psum.tile([P, BANK], F32, tag="unit", bufs=UNIT_BANKS, name="bank")
             product(bank, x_mx[c], c, w_mx[i], q, kind)
             return bank
 
@@ -263,8 +266,8 @@ def tile_continuummemorysystem_pb_kernel(tc, x_pred, W_gate, W_up, err, out):
             w_start[SLOTS * (t - 2) + 3] = t
 
         def groups(u):
-            first = u - LAG + max(0, u - (UNITS - CATCH_UP))
-            return [k for k in range(first, first + (2 if u >= UNITS - CATCH_UP else 1)) if k >= 0]
+            first = 2 * ((u - LAG) // 2) + 2 * max(0, (u - UNITS + CATCH_UP + 1) // 2)
+            return [k for k in (first, first + 1) if k >= 0 and ((u - LAG) % 2 == 0 or u >= UNITS - CATCH_UP)]
 
         waiting = None
         to_quantise = []
@@ -276,19 +279,19 @@ def tile_continuummemorysystem_pb_kernel(tc, x_pred, W_gate, W_up, err, out):
             slot = c * CHUNKS + q
             if u == 1:
                 up_bank = unit_product(u, 1)
-                w_banks = [transpose_rows(w_rows[1][b], "trans") for b in range(2)]
+                w_banks = [transpose_rows(w_rows[1][b], "side") for b in range(2)]
             if u + 1 < UNITS:
                 gate_bank = unit_product(u + 1, 0)
             if u in w_start and u > 1:
-                w_banks = [transpose_rows(w_rows[w_start[u]][b], "trans") for b in range(2)]
+                w_banks = [transpose_rows(w_rows[w_start[u]][b], "side") for b in range(2)]
             for k in groups(u):
                 second_group(k)
-            if u == 10:
+            if u == 8:
                 surprise_scale()
             if u != 1:
                 up_bank = unit_product(u, 1)
-            if 2 <= u < 8:
-                add_squares(32 * (u - 2) // 6, 32 * (u - 1) // 6)
+            if 2 <= u < 6:
+                add_squares(32 * (u - 2) // 4, 32 * (u - 1) // 4)
             ready = to_quantise
             if u != 1:
                 next_silu = unit_silu(gate_bank) if u + 1 < UNITS else None
@@ -301,15 +304,16 @@ def tile_continuummemorysystem_pb_kernel(tc, x_pred, W_gate, W_up, err, out):
                     evacuate(k // FEATURE_TILES, 0, False)
             if u == 1:
                 next_silu = unit_silu(gate_bank)
-            if 3 <= u < 7:
+            if 3 <= u < 3 + 4:
                 interleave_err(1, u - 3, 4)
+            if 3 <= u < 3 + 4:
                 interleave_err(0, u - 3, 4)
             for k in groups(u):
                 if k % FEATURE_TILES == 3:
                     evacuate(k // FEATURE_TILES, 1, True)
             if q == 0:
                 h_grouped = stage.tile([P, RANGE, PACK], BF16, tag="h_grouped", align_bytes=64)
-            if u == 8:
+            if u == 6:
                 nc.vector.tensor_tensor(out=diagonal[:], in0=identity[:], in1=gram[0][:, 0:P], op=ALU.mult)
             for grouped, t, b in ready:
                 quantise_half(grouped, w_mx[t], b)
@@ -324,13 +328,13 @@ def tile_continuummemorysystem_pb_kernel(tc, x_pred, W_gate, W_up, err, out):
                 quantise_h(*waiting)
             waiting = (h_grouped, i, c)
             if u in (8, 9):
-                c_err = u - 8
+                c_err = (8, 9).index(u)
                 quantise(err_grouped[c_err][:].rearrange("p d r -> p (d r)"), err_mx[c_err][0][:], err_mx[c_err][1][:])
         for k in range(UNITS - LAG + CATCH_UP, LAST * FEATURE_TILES):
-            second_group(k, "trans" if k >= LAST * FEATURE_TILES - 2 else "out")
-            if k % FEATURE_TILES == 1:
-                evacuate(k // FEATURE_TILES, 0, False)
-        last_banks = [psum.tile([P, BANK], F32, tag=("trans", "gate", "gate", "out")[f], name="last_bank%d" % f) for f in range(FEATURE_TILES)]
+            second_group(k, "side" if k >= LAST * FEATURE_TILES - 2 else "side")
+            if k % 2 == 1 and k < LAST * FEATURE_TILES - 1:
+                evacuate(k // FEATURE_TILES, k % FEATURE_TILES // 2, False)
+        last_banks = [psum.tile([P, BANK], F32, tag=("side", "unit", "unit", "unit")[f], bufs=(3, UNIT_BANKS, UNIT_BANKS, UNIT_BANKS)[f], name="last_bank%d" % f) for f in range(FEATURE_TILES)]
         for f in range(FEATURE_TILES):
             second_pass(last_banks[f][:, 0:RANGE], LAST, 0, f)
         quantise_h(*waiting)

@@ -29,8 +29,12 @@ FEATURE_TILES = FEATURES // P
 SLOTS = TOKEN_PASSES * CHUNKS
 CATCH_UP = 4
 WARM = 4
+GRAM = {1: (0, 8), 2: (8, 16), 5: (16, 24), 6: (24, 32)}
+ERR_PIECES = {1: ((0, 0), (0, 2)), 2: ((0, 1), (0, 3)), 4: ((1, 0), (1, 2)), 5: ((1, 1), (1, 3))}
+ON_VECTOR = {(0, 0), (0, 1), (1, 0), (1, 1)}
+QERR = {4: 0, 8: 1}
 UNIT_BANKS = 5
-BUFS = {"side": 3, "unit": UNIT_BANKS}
+BUFS = {"unit": UNIT_BANKS, "side0": 1, "side1": 1, "side2": 1}
 LAG = 12
 
 FLOPS = 2 * TOKENS * FEATURES * 2 * HIDDEN + 2 * FEATURES * TOKENS * HIDDEN
@@ -56,6 +60,13 @@ def tile_continuummemorysystem_pb_kernel(tc, x_pred, W_gate, W_up, err, out):
         warm = keep.tile([P, BANK], BF16)
         nc.vector.memset(warm[:], 0.0)
 
+        side_count = []
+
+        def side():
+            k = len(side_count)
+            side_count.append(k)
+            return "side%d" % (k % 2 if k < 10 else (k - 8) % 3)
+
         def load(view, slots, name):
             rows = keep.tile([P, slots, FEATURES], BF16, name=name)
             nc.sync.dma_start(out=rows[:], in_=view)
@@ -75,11 +86,13 @@ def tile_continuummemorysystem_pb_kernel(tc, x_pred, W_gate, W_up, err, out):
             view = err[c * K_PASS : (c + 1) * K_PASS, :].rearrange("(p r) d -> p r d", r=PACK)
             return load(view, PACK, "err_rows%d" % c)
 
-        x_rows = [load_x(0)]
-        w_rows = [load_w(0)]
+        x_rows, w_rows, err_rows = [], [], []
+        x_rows.append(load_x(0))
+        w_rows.append(load_w(0))
         x_rows.append(load_x(1))
+        err_rows.append(load_err(0))
         w_rows.append(load_w(1))
-        err_rows = [load_err(c) for c in range(TOKEN_PASSES)]
+        err_rows.append(load_err(1))
         for i in range(2, RANGES):
             w_rows.append(load_w(i))
 
@@ -121,7 +134,7 @@ def tile_continuummemorysystem_pb_kernel(tc, x_pred, W_gate, W_up, err, out):
         warm_bank = psum.tile([P, BANK], F32, tag="unit", bufs=UNIT_BANKS, name="warm_bank")
         for i in range(WARM):
             nc.tensor.matmul(out=warm_bank[:], lhsT=warm[:, 0:P], rhs=warm[:], start=True, stop=True)
-        x0 = [transpose_rows(x_rows[0][b], "side") for b in range(2)]
+        x0 = [transpose_rows(x_rows[0][b], side()) for b in range(2)]
         x0_grouped = [copy_out(x0[b], b == 0) for b in range(2)]
         w0 = [transpose_rows(w_rows[0][b], "unit") for b in range(2)]
         x1 = [transpose_rows(x_rows[1][b], "unit") for b in range(2)]
@@ -141,7 +154,7 @@ def tile_continuummemorysystem_pb_kernel(tc, x_pred, W_gate, W_up, err, out):
             d = piece * width
             dst = err_grouped[c][:, d : d + width, :]
             src = err_rows[c][:, :, d : d + width].rearrange("p r d -> p d r")
-            if c == 0:
+            if (c, piece) in ON_VECTOR:
                 nc.vector.tensor_copy(out=dst, in_=src)
             else:
                 nc.scalar.copy(out=dst, in_=src)
@@ -151,7 +164,7 @@ def tile_continuummemorysystem_pb_kernel(tc, x_pred, W_gate, W_up, err, out):
 
         def add_squares(first, last):
             if not gram:
-                gram.append(psum.tile([P, BANK], F32, tag="side", bufs=3, name="gram"))
+                gram.append(psum.tile([P, BANK], F32, tag="side2", name="gram"))
             for k in range(first, last):
                 c, r, f = gram_blocks[k]
                 block = err_rows[c][:, r, f * P : (f + 1) * P]
@@ -205,6 +218,15 @@ def tile_continuummemorysystem_pb_kernel(tc, x_pred, W_gate, W_up, err, out):
             quantise(h_grouped[:].rearrange("p m j -> p (m j)"), codes[:], scales[:])
             h_mx[(i, c)] = (codes, scales)
 
+        def quantise_last_h(h_grouped, q):
+            if q == 0:
+                codes = stage.tile([P, RANGE], U32, tag="h_codes", bufs=10, align_bytes=64)
+                scales = stage.tile([P, RANGE], U8, tag="h_scales", bufs=10, align_bytes=64)
+                h_mx[(RANGES - 1, 1)] = (codes, scales)
+            codes, scales = h_mx[(RANGES - 1, 1)]
+            columns = slice(q * P, (q + 1) * P)
+            quantise(h_grouped[:, columns, :].rearrange("p m j -> p (m j)"), codes[:, columns], scales[:, columns])
+
         def second_pass(target, i, c, f):
             err_codes, err_scales = err_mx[c]
             h_codes, h_scales = h_mx[(i, c)]
@@ -220,11 +242,11 @@ def tile_continuummemorysystem_pb_kernel(tc, x_pred, W_gate, W_up, err, out):
 
         out_banks = {}
 
-        def second_group(k, tag="side"):
+        def second_group(k):
             i, f = divmod(k, FEATURE_TILES)
             b, half_bank = divmod(f, 2)
             if half_bank == 0:
-                out_banks[(i, b)] = psum.tile([P, BANK], F32, tag=tag, bufs=BUFS[tag], name="out_bank")
+                out_banks[(i, b)] = psum.tile([P, BANK], F32, tag=side(), name="out_bank")
             for c in range(TOKEN_PASSES):
                 second_pass(out_banks[(i, b)][:, half_bank * RANGE : (half_bank + 1) * RANGE], i, c, f)
 
@@ -235,7 +257,7 @@ def tile_continuummemorysystem_pb_kernel(tc, x_pred, W_gate, W_up, err, out):
                 nc.scalar.activation(out=dst, in_=src, func=ACT.Copy, scale=scale[:, 0:1])
 
         def evacuate(i, b, on_vector):
-            result = stage.tile([P, 2, P, CHUNKS], F32, tag="result", bufs=4)
+            result = stage.tile([P, 2, P, CHUNKS], F32, tag="result", bufs=8)
             src = out_banks[(i, b)][:].rearrange("p (f q m) -> p f m q", f=2, q=CHUNKS)
             scaled(result[:], src, on_vector)
             nc.sync.dma_start(
@@ -279,19 +301,19 @@ def tile_continuummemorysystem_pb_kernel(tc, x_pred, W_gate, W_up, err, out):
             slot = c * CHUNKS + q
             if u == 1:
                 up_bank = unit_product(u, 1)
-                w_banks = [transpose_rows(w_rows[1][b], "side") for b in range(2)]
+                w_banks = [transpose_rows(w_rows[1][b], side()) for b in range(2)]
             if u + 1 < UNITS:
                 gate_bank = unit_product(u + 1, 0)
             if u in w_start and u > 1:
-                w_banks = [transpose_rows(w_rows[w_start[u]][b], "side") for b in range(2)]
+                w_banks = [transpose_rows(w_rows[w_start[u]][b], side()) for b in range(2)]
             for k in groups(u):
                 second_group(k)
-            if u == 8:
+            if u == 9:
                 surprise_scale()
             if u != 1:
                 up_bank = unit_product(u, 1)
-            if 2 <= u < 6:
-                add_squares(32 * (u - 2) // 4, 32 * (u - 1) // 4)
+            if u in GRAM:
+                add_squares(*GRAM[u])
             ready = to_quantise
             if u != 1:
                 next_silu = unit_silu(gate_bank) if u + 1 < UNITS else None
@@ -300,20 +322,19 @@ def tile_continuummemorysystem_pb_kernel(tc, x_pred, W_gate, W_up, err, out):
                 if (u if w_start.get(u) == 1 else u - b) in w_start and not (b == 1 and u == 2):
                     to_quantise.append((copy_out(w_banks[b], u == 1 and b == 1), w_start[u if u == 1 else u - b], b))
             for k in groups(u):
-                if k % FEATURE_TILES == 1:
-                    evacuate(k // FEATURE_TILES, 0, False)
+                if k % FEATURE_TILES == 1 or (k % 2 == 1 and u >= 28):
+                    evacuate(k // FEATURE_TILES, k % FEATURE_TILES // 2, False)
             if u == 1:
                 next_silu = unit_silu(gate_bank)
-            if 3 <= u < 3 + 4:
-                interleave_err(1, u - 3, 4)
-            if 3 <= u < 3 + 4:
-                interleave_err(0, u - 3, 4)
+            for c_err, piece in ERR_PIECES.get(u, ()):
+                if (c_err, piece) not in ON_VECTOR:
+                    interleave_err(c_err, piece, 4)
             for k in groups(u):
-                if k % FEATURE_TILES == 3:
+                if k % FEATURE_TILES == 3 and u < 28:
                     evacuate(k // FEATURE_TILES, 1, True)
             if q == 0:
                 h_grouped = stage.tile([P, RANGE, PACK], BF16, tag="h_grouped", align_bytes=64)
-            if u == 6:
+            if u == 7:
                 nc.vector.tensor_tensor(out=diagonal[:], in0=identity[:], in1=gram[0][:, 0:P], op=ALU.mult)
             for grouped, t, b in ready:
                 quantise_half(grouped, w_mx[t], b)
@@ -324,20 +345,25 @@ def tile_continuummemorysystem_pb_kernel(tc, x_pred, W_gate, W_up, err, out):
                 op=ALU.mult,
             )
             silu = next_silu
+            if u == UNITS - 1:
+                quantise_last_h(h_grouped, 0)
             if q == 0 and waiting is not None:
                 quantise_h(*waiting)
             waiting = (h_grouped, i, c)
-            if u in (8, 9):
-                c_err = (8, 9).index(u)
+            for c_err, piece in ERR_PIECES.get(u, ()):
+                if (c_err, piece) in ON_VECTOR:
+                    interleave_err(c_err, piece, 4)
+            if u in QERR:
+                c_err = QERR[u]
                 quantise(err_grouped[c_err][:].rearrange("p d r -> p (d r)"), err_mx[c_err][0][:], err_mx[c_err][1][:])
         for k in range(UNITS - LAG + CATCH_UP, LAST * FEATURE_TILES):
-            second_group(k, "side" if k >= LAST * FEATURE_TILES - 2 else "side")
+            second_group(k)
             if k % 2 == 1 and k < LAST * FEATURE_TILES - 1:
                 evacuate(k // FEATURE_TILES, k % FEATURE_TILES // 2, False)
-        last_banks = [psum.tile([P, BANK], F32, tag=("side", "unit", "unit", "unit")[f], bufs=(3, UNIT_BANKS, UNIT_BANKS, UNIT_BANKS)[f], name="last_bank%d" % f) for f in range(FEATURE_TILES)]
+        last_banks = [psum.tile([P, BANK], F32, tag="unit" if f else side(), bufs=UNIT_BANKS if f else 1, name="last_bank%d" % f) for f in range(FEATURE_TILES)]
         for f in range(FEATURE_TILES):
             second_pass(last_banks[f][:, 0:RANGE], LAST, 0, f)
-        quantise_h(*waiting)
+        quantise_last_h(h_grouped, 1)
         evacuate(LAST - 1, 1, False)
         for f in range(FEATURE_TILES):
             second_pass(last_banks[f][:, 0:RANGE], LAST, 1, f)

@@ -152,8 +152,8 @@ def tile_continuummemorysystem_pb_kernel(tc, x_pred, W_gate, W_up, err, out):
         def interleave_err(c, piece, pieces):
             width = FEATURES // pieces
             d = piece * width
-            dst = err_grouped[c][:, d : d + width, :]
-            src = err_rows[c][:, :, d : d + width].rearrange("p r d -> p d r")
+            dst = err_grouped[c][:, d : d + width, :].rearrange("p (g i) r -> p g r i", i=4)
+            src = err_rows[c][:, :, d : d + width].rearrange("p r (g i) -> p g r i", i=4)
             if (c, piece) in ON_VECTOR:
                 nc.vector.tensor_copy(out=dst, in_=src)
             else:

from contextlib import ExitStack

import concourse.mybir as mybir
from concourse.masks import make_identity

F32 = mybir.dt.float32
BF16 = mybir.dt.bfloat16
U32 = mybir.dt.uint32
U8 = mybir.dt.uint8
FP8X4 = mybir.dt.float8_e4m3fn_x4
ACT = mybir.ActivationFunctionType
ALU = mybir.AluOpType
AXIS = mybir.AxisListType

P = 128
PACK = 4
K_PASS = P * PACK
BANK = 512

TOKENS = 1024
FEATURES = 512
HIDDEN = 2048

TOKEN_PASSES = TOKENS // K_PASS
RANGE = 2 * P
RANGES = HIDDEN // RANGE
CHUNKS = RANGE // P
FEATURE_TILES = FEATURES // P
SLOTS = TOKEN_PASSES * CHUNKS
CATCH_UP = 4
WARM = 4
GRAM = {1: (0, 8), 2: (8, 16), 5: (16, 24), 6: (24, 32)}
ERR_PIECES = {1: ((0, 0), (0, 2)), 2: ((0, 1), (0, 3)), 4: ((1, 0), (1, 2)), 5: ((1, 1), (1, 3))}
ON_VECTOR = {(0, 0), (0, 1), (1, 0), (1, 1)}
QERR = {4: 0, 8: 1}
UNIT_BANKS = 5
BUFS = {"unit": UNIT_BANKS, "side0": 1, "side1": 1, "side2": 1}
LAG = 12

FLOPS = 2 * TOKENS * FEATURES * 2 * HIDDEN + 2 * FEATURES * TOKENS * HIDDEN


def tile_continuummemorysystem_pb_kernel(tc, x_pred, W_gate, W_up, err, out):
    nc = tc.nc
    with ExitStack() as ctx:
        ctx.enter_context(tc.manual_schedule())
        keep = ctx.enter_context(tc.tile_pool(name="keep", bufs=1))
        stage = ctx.enter_context(tc.tile_pool(name="stage", bufs=4))
        psum = ctx.enter_context(tc.psum_pool(name="psum", bufs=1))

        identity = keep.tile([P, P], F32)
        make_identity(nc, identity[:])
        ones = keep.tile([P, P], F32)
        nc.gpsimd.memset(ones[:], 1.0)
        half = keep.tile([P, 1], F32)
        nc.gpsimd.memset(half[:], 0.5)
        minus_one = keep.tile([P, 1], F32)
        nc.gpsimd.memset(minus_one[:], -1.0)

        warm = keep.tile([P, BANK], BF16)
        nc.vector.memset(warm[:], 0.0)

        side_count = []

        def side():
            k = len(side_count)
            side_count.append(k)
            return "side%d" % (k % 2 if k < 10 else (k - 8) % 3)

        def load(view, slots, name):
            rows = keep.tile([P, slots, FEATURES], BF16, name=name)
            nc.sync.dma_start(out=rows[:], in_=view)
            return rows

        def load_x(c):
            view = x_pred[c * K_PASS : (c + 1) * K_PASS, :].rearrange("(p r) d -> p r d", r=PACK)
            return [load(view[:, 2 * b : 2 * b + 2, :], 2, "x_rows%d_%d" % (c, b)) for b in range(2)]

        def load_w(i):
            return [
                load(weight[i * RANGE : (i + 1) * RANGE, :].rearrange("(p r) d -> p r d", r=CHUNKS), CHUNKS, "w_rows%d_%d" % (i, kind))
                for kind, weight in enumerate((W_gate, W_up))
            ]

        def load_err(c):
            view = err[c * K_PASS : (c + 1) * K_PASS, :].rearrange("(p r) d -> p r d", r=PACK)
            return load(view, PACK, "err_rows%d" % c)

        x_rows, w_rows, err_rows = [], [], []
        x_rows.append(load_x(0))
        w_rows.append(load_w(0))
        x_rows.append(load_x(1))
        err_rows.append(load_err(0))
        w_rows.append(load_w(1))
        err_rows.append(load_err(1))
        for i in range(2, RANGES):
            w_rows.append(load_w(i))

        def transpose_rows(rows, tag):
            words = rows[:].rearrange("p r d -> p (r d)").bitcast(F32)
            bank = psum.tile([P, BANK], F32, tag=tag, bufs=BUFS[tag], name="bank")
            for i in range(BANK // P):
                nc.tensor.transpose(
                    out=bank[:, i * P : (i + 1) * P], in_=words[:, i * P : (i + 1) * P], identity=identity[:]
                )
            return bank

        def copy_out(bank, on_vector):
            grouped = stage.tile([P, BANK * 2], BF16, tag="grouped", name="grouped", align_bytes=64)
            src = bank[:].rearrange("p (a u m) -> p a m u", a=2, u=2)
            dst = grouped[:].bitcast(F32).rearrange("p (a m u) -> p a m u", a=2, u=2)
            if on_vector:
                nc.vector.tensor_copy(out=dst, in_=src)
            else:
                nc.scalar.copy(out=dst, in_=src)
            return grouped

        def quantise(grouped, codes, scales):
            nc.vector.quantize_mx(out=codes.bitcast(FP8X4), scales=scales, in_=grouped)

        def code_tiles(name):
            codes = keep.tile([P, BANK], U32, name=name + "_codes", align_bytes=64)
            scales = keep.tile([P, BANK], U8, name=name + "_scales", align_bytes=64)
            return codes, scales

        x_mx = [code_tiles("x%d" % c) for c in range(TOKEN_PASSES)]
        w_mx = [code_tiles("w%d" % i) for i in range(RANGES)]
        err_mx = [code_tiles("err%d" % c) for c in range(TOKEN_PASSES)]

        def quantise_half(grouped, pair, b):
            codes, scales = pair
            quantise(grouped[:], codes[:, b * RANGE : (b + 1) * RANGE], scales[:, b * RANGE : (b + 1) * RANGE])

        warm_bank = psum.tile([P, BANK], F32, tag="unit", bufs=UNIT_BANKS, name="warm_bank")
        for i in range(WARM):
            nc.tensor.matmul(out=warm_bank[:], lhsT=warm[:, 0:P], rhs=warm[:], start=True, stop=True)
        x0 = [transpose_rows(x_rows[0][b], side()) for b in range(2)]
        x0_grouped = [copy_out(x0[b], b == 0) for b in range(2)]
        w0 = [transpose_rows(w_rows[0][b], "unit") for b in range(2)]
        x1 = [transpose_rows(x_rows[1][b], "unit") for b in range(2)]
        w0_grouped = [copy_out(w0[b], False) for b in range(2)]
        for b in range(2):
            quantise_half(x0_grouped[b], x_mx[0], b)
        quantise_half(w0_grouped[0], w_mx[0], 0)
        x1_grouped = [copy_out(x1[b], b == 0) for b in range(2)]
        quantise_half(w0_grouped[1], w_mx[0], 1)
        for b in range(2):
            quantise_half(x1_grouped[b], x_mx[1], b)

        err_grouped = [stage.tile([P, FEATURES, PACK], BF16, tag="err_grouped", name="err_grouped%d" % c, align_bytes=64) for c in range(TOKEN_PASSES)]

        def interleave_err(c, piece, pieces):
            width = FEATURES // pieces
            d = piece * width
            dst = err_grouped[c][:, d : d + width, :].rearrange("p (g i) r -> p g r i", i=4)
            src = err_rows[c][:, :, d : d + width].rearrange("p r (g i) -> p g r i", i=4)
            if (c, piece) in ON_VECTOR:
                nc.vector.tensor_copy(out=dst, in_=src)
            else:
                nc.scalar.copy(out=dst, in_=src)

        gram_blocks = [(c, r, f) for c in range(TOKEN_PASSES) for r in range(PACK) for f in range(FEATURE_TILES)]
        gram = []

        def add_squares(first, last):
            if not gram:
                gram.append(psum.tile([P, BANK], F32, tag="side2", name="gram"))
            for k in range(first, last):
                c, r, f = gram_blocks[k]
                block = err_rows[c][:, r, f * P : (f + 1) * P]
                nc.tensor.matmul(
                    out=gram[0][:, 0:P], lhsT=block, rhs=block, start=(k == 0), stop=(k == len(gram_blocks) - 1)
                )

        diagonal = keep.tile([P, P], F32)
        scale = keep.tile([P, 1], F32)

        def surprise_scale():
            sums_bank = psum.tile([P, BANK], F32, tag="unit", bufs=UNIT_BANKS, name="sums_bank")
            column_sums = sums_bank[:, 0:P]
            nc.tensor.matmul(out=column_sums, lhsT=ones[:], rhs=diagonal[:], start=True, stop=True)
            total = keep.tile([P, 1], F32)
            nc.vector.tensor_reduce(out=total[:], in_=column_sums, axis=AXIS.X, op=ALU.add)
            root = keep.tile([P, 1], F32)
            nc.gpsimd.tensor_tensor(out=root[:], in0=total[:], in1=half[:], op=ALU.pow)
            ema = keep.tile([P, 1], F32)
            nc.gpsimd.tensor_scalar(
                out=ema[:], in0=root[:], scalar1=0.05 / TOKENS, scalar2=0.95, op0=ALU.mult, op1=ALU.add
            )
            inverse = keep.tile([P, 1], F32)
            nc.gpsimd.tensor_tensor(out=inverse[:], in0=ema[:], in1=minus_one[:], op=ALU.pow)
            ratio = keep.tile([P, 1], F32)
            nc.gpsimd.tensor_tensor(out=ratio[:], in0=root[:], in1=inverse[:], op=ALU.mult)
            nc.gpsimd.tensor_scalar(
                out=scale[:], in0=ratio[:], scalar1=1.0 / TOKENS**2, scalar2=3.0 / TOKENS, op0=ALU.mult, op1=ALU.min
            )

        def product(bank, pair, c, w, q, kind):
            codes, scales = w
            x_codes, x_scales = pair
            first = kind * RANGE + q * P
            for j in range(PACK):
                nc.tensor.matmul_mx(
                    out=bank[:, j * P : (j + 1) * P],
                    lhsT=x_codes[:, j * P : (j + 1) * P].bitcast(FP8X4),
                    lhsT_scale=x_scales[:, j * P : (j + 1) * P],
                    rhs=codes[:, first : first + P].bitcast(FP8X4),
                    rhs_scale=scales[:, first : first + P],
                    start=True,
                    stop=True,
                )

        h_mx = {}

        def quantise_h(h_grouped, i, c):
            codes = stage.tile([P, RANGE], U32, tag="h_codes", bufs=10, align_bytes=64)
            scales = stage.tile([P, RANGE], U8, tag="h_scales", bufs=10, align_bytes=64)
            quantise(h_grouped[:].rearrange("p m j -> p (m j)"), codes[:], scales[:])
            h_mx[(i, c)] = (codes, scales)

        def quantise_last_h(h_grouped, q):
            if q == 0:
                codes = stage.tile([P, RANGE], U32, tag="h_codes", bufs=10, align_bytes=64)
                scales = stage.tile([P, RANGE], U8, tag="h_scales", bufs=10, align_bytes=64)
                h_mx[(RANGES - 1, 1)] = (codes, scales)
            codes, scales = h_mx[(RANGES - 1, 1)]
            columns = slice(q * P, (q + 1) * P)
            quantise(h_grouped[:, columns, :].rearrange("p m j -> p (m j)"), codes[:, columns], scales[:, columns])

        def second_pass(target, i, c, f):
            err_codes, err_scales = err_mx[c]
            h_codes, h_scales = h_mx[(i, c)]
            nc.tensor.matmul_mx(
                out=target,
                lhsT=err_codes[:, f * P : (f + 1) * P].bitcast(FP8X4),
                lhsT_scale=err_scales[:, f * P : (f + 1) * P],
                rhs=h_codes[:].bitcast(FP8X4),
                rhs_scale=h_scales[:],
                start=(c == 0),
                stop=(c == TOKEN_PASSES - 1),
            )

        out_banks = {}

        def second_group(k):
            i, f = divmod(k, FEATURE_TILES)
            b, half_bank = divmod(f, 2)
            if half_bank == 0:
                out_banks[(i, b)] = psum.tile([P, BANK], F32, tag=side(), name="out_bank")
            for c in range(TOKEN_PASSES):
                second_pass(out_banks[(i, b)][:, half_bank * RANGE : (half_bank + 1) * RANGE], i, c, f)

        def scaled(dst, src, on_vector):
            if on_vector:
                nc.vector.tensor_scalar_mul(out=dst, in0=src, scalar1=scale[:, 0:1])
            else:
                nc.scalar.activation(out=dst, in_=src, func=ACT.Copy, scale=scale[:, 0:1])

        def evacuate(i, b, on_vector):
            result = stage.tile([P, 2, P, CHUNKS], F32, tag="result", bufs=8)
            src = out_banks[(i, b)][:].rearrange("p (f q m) -> p f m q", f=2, q=CHUNKS)
            scaled(result[:], src, on_vector)
            nc.sync.dma_start(
                out=out[2 * b * P : 2 * (b + 1) * P, i * RANGE : (i + 1) * RANGE].rearrange("(f p) n -> p f n", f=2),
                in_=result[:].rearrange("p f m q -> p f (m q)"),
            )

        UNITS = RANGES * SLOTS
        LAST = RANGES - 1

        def place(u):
            i, slot = divmod(u, SLOTS)
            return (i,) + divmod(slot, CHUNKS)

        def unit_product(u, kind):
            i, c, q = place(u)
            bank = psum.tile([P, BANK], F32, tag="unit", bufs=UNIT_BANKS, name="bank")
            product(bank, x_mx[c], c, w_mx[i], q, kind)
            return bank

        def unit_silu(bank):
            silu = stage.tile([P, P, PACK], F32, tag="silu", name="silu")
            nc.scalar.activation(out=silu[:], in_=bank[:].rearrange("p (j m) -> p m j", j=PACK), func=ACT.Silu)
            return silu

        w_start = {1: 1}
        for t in range(2, RANGES):
            w_start[SLOTS * (t - 2) + 3] = t

        def groups(u):
            first = 2 * ((u - LAG) // 2) + 2 * max(0, (u - UNITS + CATCH_UP + 1) // 2)
            return [k for k in (first, first + 1) if k >= 0 and ((u - LAG) % 2 == 0 or u >= UNITS - CATCH_UP)]

        waiting = None
        to_quantise = []
        w_banks = []
        gate_bank = unit_product(0, 0)
        silu = unit_silu(gate_bank)
        for u in range(UNITS):
            i, c, q = place(u)
            slot = c * CHUNKS + q
            if u == 1:
                up_bank = unit_product(u, 1)
                w_banks = [transpose_rows(w_rows[1][b], side()) for b in range(2)]
            if u + 1 < UNITS:
                gate_bank = unit_product(u + 1, 0)
            if u in w_start and u > 1:
                w_banks = [transpose_rows(w_rows[w_start[u]][b], side()) for b in range(2)]
            for k in groups(u):
                second_group(k)
            if u == 9:
                surprise_scale()
            if u != 1:
                up_bank = unit_product(u, 1)
            if u in GRAM:
                add_squares(*GRAM[u])
            ready = to_quantise
            if u != 1:
                next_silu = unit_silu(gate_bank) if u + 1 < UNITS else None
            to_quantise = []
            for b in range(2):
                if (u if w_start.get(u) == 1 else u - b) in w_start and not (b == 1 and u == 2):
                    to_quantise.append((copy_out(w_banks[b], u == 1 and b == 1), w_start[u if u == 1 else u - b], b))
            for k in groups(u):
                if k % FEATURE_TILES == 1 or (k % 2 == 1 and u >= 28):
                    evacuate(k // FEATURE_TILES, k % FEATURE_TILES // 2, False)
            if u == 1:
                next_silu = unit_silu(gate_bank)
            for c_err, piece in ERR_PIECES.get(u, ()):
                if (c_err, piece) not in ON_VECTOR:
                    interleave_err(c_err, piece, 4)
            for k in groups(u):
                if k % FEATURE_TILES == 3 and u < 28:
                    evacuate(k // FEATURE_TILES, 1, True)
            if q == 0:
                h_grouped = stage.tile([P, RANGE, PACK], BF16, tag="h_grouped", align_bytes=64)
            if u == 7:
                nc.vector.tensor_tensor(out=diagonal[:], in0=identity[:], in1=gram[0][:, 0:P], op=ALU.mult)
            for grouped, t, b in ready:
                quantise_half(grouped, w_mx[t], b)
            nc.vector.tensor_tensor(
                out=h_grouped[:, q * P : (q + 1) * P, :],
                in0=silu[:],
                in1=up_bank[:].rearrange("p (j m) -> p m j", j=PACK),
                op=ALU.mult,
            )
            silu = next_silu
            if u == UNITS - 1:
                quantise_last_h(h_grouped, 0)
            if q == 0 and waiting is not None:
                quantise_h(*waiting)
            waiting = (h_grouped, i, c)
            for c_err, piece in ERR_PIECES.get(u, ()):
                if (c_err, piece) in ON_VECTOR:
                    interleave_err(c_err, piece, 4)
            if u in QERR:
                c_err = QERR[u]
                quantise(err_grouped[c_err][:].rearrange("p d r -> p (d r)"), err_mx[c_err][0][:], err_mx[c_err][1][:])
        for k in range(UNITS - LAG + CATCH_UP, LAST * FEATURE_TILES):
            second_group(k)
            if k % 2 == 1 and k < LAST * FEATURE_TILES - 1:
                evacuate(k // FEATURE_TILES, k % FEATURE_TILES // 2, False)
        last_banks = [psum.tile([P, BANK], F32, tag="unit" if f else side(), bufs=UNIT_BANKS if f else 1, name="last_bank%d" % f) for f in range(FEATURE_TILES)]
        for f in range(FEATURE_TILES):
            second_pass(last_banks[f][:, 0:RANGE], LAST, 0, f)
        quantise_last_h(h_grouped, 1)
        evacuate(LAST - 1, 1, False)
        for f in range(FEATURE_TILES):
            second_pass(last_banks[f][:, 0:RANGE], LAST, 1, f)
        for f in range(FEATURE_TILES):
            result = stage.tile([P, P, CHUNKS], F32, tag="last_result")
            scaled(result[:], last_banks[f][:, 0:RANGE].rearrange("p (q m) -> p m q", q=CHUNKS), f % 2 == 1)
            nc.sync.dma_start(
                out=out[f * P : (f + 1) * P, LAST * RANGE : (LAST + 1) * RANGE],
                in_=result[:].rearrange("p m q -> p (m q)"),
            )
